import numpy as np
import ml_dtypes

BF16 = ml_dtypes.bfloat16


def bf(x):
    return np.asarray(x, np.float32).astype(BF16)


def f32(x):
    return np.asarray(x, np.float32)


def f64(x):
    return np.asarray(x).astype(np.float64)


def striped(idx):
    return np.tile(idx.reshape(-1, 16).T, (8, 1))


C, S, N, K, TS, U, R = 1024, 512, 1024, 2, 128, 8, 256


def setup_inputs():
    return {"x": f32(bf(np.random.standard_normal((C, S)))), "v": f32(0.25 * np.random.standard_normal((N, R))), "offs": striped(np.concatenate([np.random.permutation(S) for _ in range(K)]))}


def reference(x, v, offs):
    idx = offs[:16].T.reshape(-1)
    vv = f64(v).reshape(U, TS, R)
    vn = vv / np.sqrt(np.sum(vv * vv, axis=1, keepdims=True))
    xt = f64(x)[:, idx].reshape(C, U, TS)
    return np.einsum('cut,utr->cur', xt, vn).reshape(C, U * R)

@@ -1,0 +1,116 @@
+import concourse.mybir as mybir
+from concourse.masks import make_identity
+
+F32 = mybir.dt.float32
+BF16 = mybir.dt.bfloat16
+U16 = mybir.dt.uint16
+COPY = mybir.ActivationFunctionType.Copy
+INVERSE_ROOT = mybir.ActivationFunctionType.Abs_reciprocal_sqrt
+MULT = mybir.AluOpType.mult
+
+P = 128
+TOKENS, FEATURES = 1024, 512
+ENTRIES, READ_IN = 1024, 256
+BANK = 512
+PIECE = 512
+BLOCKS = TOKENS // P
+GROUPS = ENTRIES * READ_IN // (P * BANK)
+PIECES_A_BLOCK = ENTRIES // PIECE
+GROUPS_A_PIECE = GROUPS // PIECES_A_BLOCK
+TILES_A_GROUP = BANK // READ_IN
+LOOK_UPS = BLOCKS * PIECES_A_BLOCK
+AHEAD = 2
+
+FLOPS = 2 * TOKENS * ENTRIES * READ_IN
+
+
+def tile_tiledsparseread_kernel(tc, x, v, offs, out):
+    nc = tc.nc
+    with (
+        tc.tile_pool(name="held", bufs=1) as held,
+        tc.tile_pool(name="scratch", bufs=2) as scratch,
+        tc.tile_pool(name="picked", bufs=4) as picked_pool,
+        tc.tile_pool(name="flipped", bufs=AHEAD + 2) as flipped_pool,
+        tc.tile_pool(name="staged", bufs=4) as staged_pool,
+        tc.psum_pool(name="banks", bufs=8) as banks,
+    ):
+        offsets = held.tile([P, ENTRIES // 16], U16, name="offsets")
+        nc.sync.dma_start(offsets[:], offs)
+
+        tokens = []
+        for b in range(BLOCKS):
+            window = held.tile([P, FEATURES], F32, name=f"tokens{b}")
+            nc.sync.dma_start(window[:], x[b * P : (b + 1) * P, :])
+            tokens.append(window)
+
+        raw = []
+        for g in range(GROUPS):
+            rows = v[g * TILES_A_GROUP * P : (g + 1) * TILES_A_GROUP * P, :]
+            columns = held.tile([P, BANK], F32, name=f"raw{g}")
+            nc.scalar.dma_start(
+                columns[:].rearrange("t (h r) -> t h r", h=TILES_A_GROUP),
+                rows.rearrange("(h t) r -> t h r", t=P),
+            )
+            raw.append(columns)
+
+        identity = held.tile([P, P], F32, name="identity")
+        make_identity(nc, identity[:])
+        ones = held.tile([P, P], F32, name="ones")
+        nc.vector.memset(ones[:], 1.0)
+
+        unit = []
+
+        def normalise(g):
+            squares = scratch.tile([P, BANK], F32, name="squares")
+            nc.gpsimd.tensor_tensor(squares[:], raw[g][:], raw[g][:], MULT)
+            sums = banks.tile([P, BANK], F32, name="sums", tag="bank")
+            nc.tensor.matmul(sums[:], ones[:], squares[:], start=True, stop=True)
+            inverse = scratch.tile([P, BANK], F32, name="inverse")
+            nc.scalar.activation(inverse[:], sums[:], INVERSE_ROOT)
+            columns = held.tile([P, BANK], BF16, name=f"unit{g}")
+            nc.vector.tensor_tensor(columns[:], raw[g][:], inverse[:], MULT)
+            unit.append(columns)
+
+        def look_up(b, k):
+            picked = picked_pool.tile([P, PIECE], F32, name="picked")
+            entries = offsets[:, k * PIECE // 16 : (k + 1) * PIECE // 16]
+            nc.scalar.activation(picked[:], tokens[b][:].indirect(entries), COPY)
+            turned = banks.tile([P, BANK], F32, name="turned", tag="bank")
+            for j in range(PIECE // P):
+                nc.tensor.transpose(
+                    turned[:, j * P : (j + 1) * P], picked[:, j * P : (j + 1) * P], identity[:]
+                )
+            flipped = flipped_pool.tile([P, PIECE], BF16, name="flipped")
+            nc.vector.tensor_copy(flipped[:], turned[:])
+            return flipped
+
+        def project(b, k, flipped):
+            staged = staged_pool.tile([P, GROUPS_A_PIECE * BANK], F32, name="staged")
+            for i in range(GROUPS_A_PIECE):
+                g = k * GROUPS_A_PIECE + i
+                product = banks.tile([P, BANK], F32, name="product", tag="bank")
+                for h in range(TILES_A_GROUP):
+                    j = i * TILES_A_GROUP + h
+                    nc.tensor.matmul(
+                        product[:, h * READ_IN : (h + 1) * READ_IN],
+                        flipped[:, j * P : (j + 1) * P],
+                        unit[g][:, h * READ_IN : (h + 1) * READ_IN],
+                        start=True,
+                        stop=True,
+                    )
+                if g == GROUPS - 1:
+                    nc.scalar.activation(staged[:, i * BANK : (i + 1) * BANK], product[:], COPY)
+                else:
+                    nc.vector.tensor_copy(staged[:, i * BANK : (i + 1) * BANK], product[:])
+            width = GROUPS_A_PIECE * BANK
+            nc.sync.dma_start(out[b * P : (b + 1) * P, k * width : (k + 1) * width], staged[:])
+
+        waiting = []
+        for n in range(LOOK_UPS + AHEAD):
+            if n < LOOK_UPS:
+                waiting.append(look_up(n // PIECES_A_BLOCK, n % PIECES_A_BLOCK))
+            if n < GROUPS:
+                normalise(n)
+            if n >= AHEAD:
+                m = n - AHEAD
+                project(m // PIECES_A_BLOCK, m % PIECES_A_BLOCK, waiting[m])

@@ -14,12 +14,15 @@ ENTRIES, READ_IN = 1024, 256
 BANK = 512
 PIECE = 512
 BLOCKS = TOKENS // P
-GROUPS = ENTRIES * READ_IN // (P * BANK)
 PIECES_A_BLOCK = ENTRIES // PIECE
-GROUPS_A_PIECE = GROUPS // PIECES_A_BLOCK
+GROUPS_A_PIECE = PIECE * READ_IN // (P * BANK)
+GROUPS = PIECES_A_BLOCK * GROUPS_A_PIECE
 TILES_A_GROUP = BANK // READ_IN
 LOOK_UPS = BLOCKS * PIECES_A_BLOCK
-AHEAD = 2
+FLIP_LAG = 2
+PRODUCT_LAG = 4
+SCALAR_TURN = 8
+WARM_UPS = 8
 
 FLOPS = 2 * TOKENS * ENTRIES * READ_IN
 
@@ -28,64 +31,83 @@ def tile_tiledsparseread_kernel(tc, x, v, offs, out):
     nc = tc.nc
     with (
         tc.tile_pool(name="held", bufs=1) as held,
-        tc.tile_pool(name="scratch", bufs=2) as scratch,
-        tc.tile_pool(name="picked", bufs=4) as picked_pool,
-        tc.tile_pool(name="flipped", bufs=AHEAD + 2) as flipped_pool,
-        tc.tile_pool(name="staged", bufs=4) as staged_pool,
+        tc.tile_pool(name="scratch", bufs=GROUPS) as scratch,
+        tc.tile_pool(name="picked", bufs=FLIP_LAG + 4) as picked_pool,
+        tc.tile_pool(name="flipped", bufs=PRODUCT_LAG - FLIP_LAG + 4) as flipped_pool,
+        tc.tile_pool(name="staged", bufs=8) as staged_pool,
         tc.psum_pool(name="banks", bufs=8) as banks,
     ):
         offsets = held.tile([P, ENTRIES // 16], U16, name="offsets")
         nc.sync.dma_start(offsets[:], offs)
 
-        tokens = []
+        tokens = [held.tile([P, FEATURES], F32, name=f"tokens{b}") for b in range(BLOCKS)]
+        raw = [held.tile([P, BANK], F32, name=f"raw{g}") for g in range(GROUPS)]
+
+        def load_tokens(b):
+            nc.sync.dma_start(tokens[b][:], x[b * P : (b + 1) * P, :])
+
+        def load_columns(k):
+            for g in range(k * GROUPS_A_PIECE, (k + 1) * GROUPS_A_PIECE):
+                rows = v[g * TILES_A_GROUP * P : (g + 1) * TILES_A_GROUP * P, :]
+                nc.sync.dma_start(
+                    raw[g][:].rearrange("t (h r) -> t h r", h=TILES_A_GROUP),
+                    rows.rearrange("(h t) r -> t h r", t=P),
+                )
+
         for b in range(BLOCKS):
-            window = held.tile([P, FEATURES], F32, name=f"tokens{b}")
-            nc.sync.dma_start(window[:], x[b * P : (b + 1) * P, :])
-            tokens.append(window)
+            load_tokens(b)
+            if b < PIECES_A_BLOCK:
+                load_columns(b)
 
-        raw = []
-        for g in range(GROUPS):
-            rows = v[g * TILES_A_GROUP * P : (g + 1) * TILES_A_GROUP * P, :]
-            columns = held.tile([P, BANK], F32, name=f"raw{g}")
-            nc.scalar.dma_start(
-                columns[:].rearrange("t (h r) -> t h r", h=TILES_A_GROUP),
-                rows.rearrange("(h t) r -> t h r", t=P),
-            )
-            raw.append(columns)
-
-        identity = held.tile([P, P], F32, name="identity")
+        identity = held.tile([P, P], BF16, name="identity")
         make_identity(nc, identity[:])
         ones = held.tile([P, P], F32, name="ones")
         nc.vector.memset(ones[:], 1.0)
+        unused = held.tile([P, 1], F32, name="unused")
+        nc.scalar.activation(unused[:], ones[:, 0:1], INVERSE_ROOT)
 
-        unit = []
+        zeros = held.tile([P, BANK], BF16, name="zeros")
+        nc.vector.memset(zeros[:], 0.0)
+        warmth = banks.tile([P, BANK], F32, name="warmth", tag="bank")
+        for i in range(WARM_UPS):
+            nc.tensor.matmul(warmth[:], zeros[:, 0:P], zeros[:], start=True, stop=True)
 
-        def normalise(g):
+        sums = {}
+        unit = {}
+
+        def add_up(g):
             squares = scratch.tile([P, BANK], F32, name="squares")
-            nc.gpsimd.tensor_tensor(squares[:], raw[g][:], raw[g][:], MULT)
-            sums = banks.tile([P, BANK], F32, name="sums", tag="bank")
-            nc.tensor.matmul(sums[:], ones[:], squares[:], start=True, stop=True)
-            inverse = scratch.tile([P, BANK], F32, name="inverse")
-            nc.scalar.activation(inverse[:], sums[:], INVERSE_ROOT)
-            columns = held.tile([P, BANK], BF16, name=f"unit{g}")
-            nc.vector.tensor_tensor(columns[:], raw[g][:], inverse[:], MULT)
-            unit.append(columns)
+            nc.vector.tensor_tensor(squares[:], raw[g][:], raw[g][:], MULT)
+            sums[g] = banks.tile([P, BANK], F32, name="sums", tag="bank")
+            nc.tensor.matmul(sums[g][:], ones[:], squares[:], start=True, stop=True)
 
-        def look_up(b, k):
+        def scale(k):
+            for g in range(k * GROUPS_A_PIECE, (k + 1) * GROUPS_A_PIECE):
+                inverse = scratch.tile([P, BANK], F32, name="inverse")
+                nc.scalar.activation(inverse[:], sums[g][:], INVERSE_ROOT)
+                unit[g] = held.tile([P, BANK], BF16, name=f"unit{g}")
+                nc.gpsimd.tensor_tensor(unit[g][:], raw[g][:], inverse[:], MULT)
+
+        def look_up(n):
+            b, k = n // PIECES_A_BLOCK, n % PIECES_A_BLOCK
             picked = picked_pool.tile([P, PIECE], F32, name="picked")
             entries = offsets[:, k * PIECE // 16 : (k + 1) * PIECE // 16]
             nc.scalar.activation(picked[:], tokens[b][:].indirect(entries), COPY)
-            turned = banks.tile([P, BANK], F32, name="turned", tag="bank")
+            return picked
+
+        def flip(picked):
+            halves = picked[:].bitcast(BF16).rearrange("c (j half) -> c j half", half=2)
+            turned = banks.tile([P, PIECE], BF16, name="turned", tag="bank")
             for j in range(PIECE // P):
                 nc.tensor.transpose(
-                    turned[:, j * P : (j + 1) * P], picked[:, j * P : (j + 1) * P], identity[:]
+                    turned[:, j * P : (j + 1) * P], halves[:, j * P : (j + 1) * P, 1], identity[:]
                 )
             flipped = flipped_pool.tile([P, PIECE], BF16, name="flipped")
             nc.vector.tensor_copy(flipped[:], turned[:])
             return flipped
 
-        def project(b, k, flipped):
-            staged = staged_pool.tile([P, GROUPS_A_PIECE * BANK], F32, name="staged")
+        def project(n, flipped, scalar_is_free):
+            b, k = n // PIECES_A_BLOCK, n % PIECES_A_BLOCK
             for i in range(GROUPS_A_PIECE):
                 g = k * GROUPS_A_PIECE + i
                 product = banks.tile([P, BANK], F32, name="product", tag="bank")
@@ -98,19 +120,25 @@ def tile_tiledsparseread_kernel(tc, x, v, offs, out):
                         start=True,
                         stop=True,
                     )
-                if g == GROUPS - 1:
-                    nc.scalar.activation(staged[:, i * BANK : (i + 1) * BANK], product[:], COPY)
+                staged = staged_pool.tile([P, BANK], F32, name="staged")
+                turn = 2 if scalar_is_free else SCALAR_TURN
+                if (n * GROUPS_A_PIECE + i) % turn == turn - 1:
+                    nc.scalar.activation(staged[:], product[:], COPY)
                 else:
-                    nc.vector.tensor_copy(staged[:, i * BANK : (i + 1) * BANK], product[:])
-            width = GROUPS_A_PIECE * BANK
-            nc.sync.dma_start(out[b * P : (b + 1) * P, k * width : (k + 1) * width], staged[:])
+                    nc.vector.tensor_copy(staged[:], product[:])
+                nc.sync.dma_start(out[b * P : (b + 1) * P, g * BANK : (g + 1) * BANK], staged[:])
 
-        waiting = []
-        for n in range(LOOK_UPS + AHEAD):
-            if n < LOOK_UPS:
-                waiting.append(look_up(n // PIECES_A_BLOCK, n % PIECES_A_BLOCK))
-            if n < GROUPS:
-                normalise(n)
-            if n >= AHEAD:
-                m = n - AHEAD
-                project(m // PIECES_A_BLOCK, m % PIECES_A_BLOCK, waiting[m])
+        for g in range(GROUPS):
+            add_up(g)
+
+        picked_tiles = {}
+        flipped_tiles = {}
+        for r in range(LOOK_UPS + PRODUCT_LAG):
+            if r >= PRODUCT_LAG:
+                project(r - PRODUCT_LAG, flipped_tiles[r - PRODUCT_LAG], r >= LOOK_UPS)
+            if FLIP_LAG <= r < LOOK_UPS + FLIP_LAG:
+                flipped_tiles[r - FLIP_LAG] = flip(picked_tiles[r - FLIP_LAG])
+            if r < LOOK_UPS:
+                picked_tiles[r] = look_up(r)
+            if 1 <= r <= PIECES_A_BLOCK:
+                scale(r - 1)

@@ -21,8 +21,9 @@ TILES_A_GROUP = BANK // READ_IN
 LOOK_UPS = BLOCKS * PIECES_A_BLOCK
 FLIP_LAG = 2
 PRODUCT_LAG = 4
+ROOT_LAG = 1
 SCALAR_TURN = 8
-WARM_UPS = 8
+WARM_UPS = 5
 
 FLOPS = 2 * TOKENS * ENTRIES * READ_IN
 
@@ -54,10 +55,11 @@ def tile_tiledsparseread_kernel(tc, x, v, offs, out):
                     rows.rearrange("(h t) r -> t h r", t=P),
                 )
 
-        for b in range(BLOCKS):
+        load_tokens(0)
+        load_columns(0)
+        for b in range(1, BLOCKS):
             load_tokens(b)
-            if b < PIECES_A_BLOCK:
-                load_columns(b)
+        load_columns(1)
 
         identity = held.tile([P, P], BF16, name="identity")
         make_identity(nc, identity[:])
@@ -66,30 +68,29 @@ def tile_tiledsparseread_kernel(tc, x, v, offs, out):
         unused = held.tile([P, 1], F32, name="unused")
         nc.scalar.activation(unused[:], ones[:, 0:1], INVERSE_ROOT)
 
-        zeros = held.tile([P, BANK], BF16, name="zeros")
-        nc.vector.memset(zeros[:], 0.0)
-        warmth = banks.tile([P, BANK], F32, name="warmth", tag="bank")
+        warmth = banks.tile([P, P], F32, name="warmth", tag="bank")
         for i in range(WARM_UPS):
-            nc.tensor.matmul(warmth[:], zeros[:, 0:P], zeros[:], start=True, stop=True)
+            nc.tensor.matmul(warmth[:], ones[:], ones[:], start=True, stop=True)
 
         sums = {}
         unit = {}
 
-        def add_up(g):
-            squares = scratch.tile([P, BANK], F32, name="squares")
-            nc.vector.tensor_tensor(squares[:], raw[g][:], raw[g][:], MULT)
-            sums[g] = banks.tile([P, BANK], F32, name="sums", tag="bank")
-            nc.tensor.matmul(sums[g][:], ones[:], squares[:], start=True, stop=True)
+        def add_up(k):
+            for g in range(k * GROUPS_A_PIECE, (k + 1) * GROUPS_A_PIECE):
+                squares = scratch.tile([P, BANK], F32, name="squares")
+                nc.vector.tensor_tensor(squares[:], raw[g][:], raw[g][:], MULT)
+                sums[g] = banks.tile([P, BANK], F32, name="sums", tag="bank")
+                nc.tensor.matmul(sums[g][:], ones[:], squares[:], start=True, stop=True)
 
         def scale(k):
             for g in range(k * GROUPS_A_PIECE, (k + 1) * GROUPS_A_PIECE):
                 inverse = scratch.tile([P, BANK], F32, name="inverse")
                 nc.scalar.activation(inverse[:], sums[g][:], INVERSE_ROOT)
                 unit[g] = held.tile([P, BANK], BF16, name=f"unit{g}")
-                nc.gpsimd.tensor_tensor(unit[g][:], raw[g][:], inverse[:], MULT)
+                nc.vector.tensor_tensor(unit[g][:], raw[g][:], inverse[:], MULT)
 
         def look_up(n):
-            b, k = n // PIECES_A_BLOCK, n % PIECES_A_BLOCK
+            k, b = n // BLOCKS, n % BLOCKS
             picked = picked_pool.tile([P, PIECE], F32, name="picked")
             entries = offsets[:, k * PIECE // 16 : (k + 1) * PIECE // 16]
             nc.scalar.activation(picked[:], tokens[b][:].indirect(entries), COPY)
@@ -107,7 +108,7 @@ def tile_tiledsparseread_kernel(tc, x, v, offs, out):
             return flipped
 
         def project(n, flipped, scalar_is_free):
-            b, k = n // PIECES_A_BLOCK, n % PIECES_A_BLOCK
+            k, b = n // BLOCKS, n % BLOCKS
             for i in range(GROUPS_A_PIECE):
                 g = k * GROUPS_A_PIECE + i
                 product = banks.tile([P, BANK], F32, name="product", tag="bank")
@@ -128,17 +129,16 @@ def tile_tiledsparseread_kernel(tc, x, v, offs, out):
                     nc.vector.tensor_copy(staged[:], product[:])
                 nc.sync.dma_start(out[b * P : (b + 1) * P, g * BANK : (g + 1) * BANK], staged[:])
 
-        for g in range(GROUPS):
-            add_up(g)
-
         picked_tiles = {}
         flipped_tiles = {}
         for r in range(LOOK_UPS + PRODUCT_LAG):
             if r >= PRODUCT_LAG:
                 project(r - PRODUCT_LAG, flipped_tiles[r - PRODUCT_LAG], r >= LOOK_UPS)
+            if r < LOOK_UPS and r % BLOCKS == 0:
+                add_up(r // BLOCKS)
             if FLIP_LAG <= r < LOOK_UPS + FLIP_LAG:
                 flipped_tiles[r - FLIP_LAG] = flip(picked_tiles[r - FLIP_LAG])
             if r < LOOK_UPS:
                 picked_tiles[r] = look_up(r)
-            if 1 <= r <= PIECES_A_BLOCK:
-                scale(r - 1)
+            if r < LOOK_UPS and r % BLOCKS == ROOT_LAG:
+                scale(r // BLOCKS)

@@ -21,9 +21,7 @@ TILES_A_GROUP = BANK // READ_IN
 LOOK_UPS = BLOCKS * PIECES_A_BLOCK
 FLIP_LAG = 2
 PRODUCT_LAG = 4
-ROOT_LAG = 1
 SCALAR_TURN = 8
-WARM_UPS = 5
 
 FLOPS = 2 * TOKENS * ENTRIES * READ_IN
 
@@ -55,11 +53,10 @@ def tile_tiledsparseread_kernel(tc, x, v, offs, out):
                     rows.rearrange("(h t) r -> t h r", t=P),
                 )
 
-        load_tokens(0)
-        load_columns(0)
-        for b in range(1, BLOCKS):
+        for b in range(BLOCKS):
             load_tokens(b)
-        load_columns(1)
+            if b < PIECES_A_BLOCK:
+                load_columns(b)
 
         identity = held.tile([P, P], BF16, name="identity")
         make_identity(nc, identity[:])
@@ -68,29 +65,24 @@ def tile_tiledsparseread_kernel(tc, x, v, offs, out):
         unused = held.tile([P, 1], F32, name="unused")
         nc.scalar.activation(unused[:], ones[:, 0:1], INVERSE_ROOT)
 
-        warmth = banks.tile([P, P], F32, name="warmth", tag="bank")
-        for i in range(WARM_UPS):
-            nc.tensor.matmul(warmth[:], ones[:], ones[:], start=True, stop=True)
-
         sums = {}
         unit = {}
 
-        def add_up(k):
-            for g in range(k * GROUPS_A_PIECE, (k + 1) * GROUPS_A_PIECE):
-                squares = scratch.tile([P, BANK], F32, name="squares")
-                nc.vector.tensor_tensor(squares[:], raw[g][:], raw[g][:], MULT)
-                sums[g] = banks.tile([P, BANK], F32, name="sums", tag="bank")
-                nc.tensor.matmul(sums[g][:], ones[:], squares[:], start=True, stop=True)
+        def add_up(g):
+            squares = scratch.tile([P, BANK], F32, name="squares")
+            nc.vector.tensor_tensor(squares[:], raw[g][:], raw[g][:], MULT)
+            sums[g] = banks.tile([P, BANK], F32, name="sums", tag="bank")
+            nc.tensor.matmul(sums[g][:], ones[:], squares[:], start=True, stop=True)
 
         def scale(k):
             for g in range(k * GROUPS_A_PIECE, (k + 1) * GROUPS_A_PIECE):
                 inverse = scratch.tile([P, BANK], F32, name="inverse")
                 nc.scalar.activation(inverse[:], sums[g][:], INVERSE_ROOT)
                 unit[g] = held.tile([P, BANK], BF16, name=f"unit{g}")
-                nc.vector.tensor_tensor(unit[g][:], raw[g][:], inverse[:], MULT)
+                nc.gpsimd.tensor_tensor(unit[g][:], raw[g][:], inverse[:], MULT)
 
         def look_up(n):
-            k, b = n // BLOCKS, n % BLOCKS
+            b, k = n // PIECES_A_BLOCK, n % PIECES_A_BLOCK
             picked = picked_pool.tile([P, PIECE], F32, name="picked")
             entries = offsets[:, k * PIECE // 16 : (k + 1) * PIECE // 16]
             nc.scalar.activation(picked[:], tokens[b][:].indirect(entries), COPY)
@@ -108,7 +100,7 @@ def tile_tiledsparseread_kernel(tc, x, v, offs, out):
             return flipped
 
         def project(n, flipped, scalar_is_free):
-            k, b = n // BLOCKS, n % BLOCKS
+            b, k = n // PIECES_A_BLOCK, n % PIECES_A_BLOCK
             for i in range(GROUPS_A_PIECE):
                 g = k * GROUPS_A_PIECE + i
                 product = banks.tile([P, BANK], F32, name="product", tag="bank")
@@ -129,16 +121,17 @@ def tile_tiledsparseread_kernel(tc, x, v, offs, out):
                     nc.vector.tensor_copy(staged[:], product[:])
                 nc.sync.dma_start(out[b * P : (b + 1) * P, g * BANK : (g + 1) * BANK], staged[:])
 
+        for g in range(GROUPS):
+            add_up(g)
+
         picked_tiles = {}
         flipped_tiles = {}
         for r in range(LOOK_UPS + PRODUCT_LAG):
             if r >= PRODUCT_LAG:
                 project(r - PRODUCT_LAG, flipped_tiles[r - PRODUCT_LAG], r >= LOOK_UPS)
-            if r < LOOK_UPS and r % BLOCKS == 0:
-                add_up(r // BLOCKS)
             if FLIP_LAG <= r < LOOK_UPS + FLIP_LAG:
                 flipped_tiles[r - FLIP_LAG] = flip(picked_tiles[r - FLIP_LAG])
             if r < LOOK_UPS:
                 picked_tiles[r] = look_up(r)
-            if r < LOOK_UPS and r % BLOCKS == ROOT_LAG:
-                scale(r // BLOCKS)
+            if 1 <= r <= PIECES_A_BLOCK:
+                scale(r - 1)

@@ -101,6 +101,7 @@ def tile_tiledsparseread_kernel(tc, x, v, offs, out):
 
         def project(n, flipped, scalar_is_free):
             b, k = n // PIECES_A_BLOCK, n % PIECES_A_BLOCK
+            staged = staged_pool.tile([P, GROUPS_A_PIECE * BANK], F32, name="staged")
             for i in range(GROUPS_A_PIECE):
                 g = k * GROUPS_A_PIECE + i
                 product = banks.tile([P, BANK], F32, name="product", tag="bank")
@@ -113,13 +114,13 @@ def tile_tiledsparseread_kernel(tc, x, v, offs, out):
                         start=True,
                         stop=True,
                     )
-                staged = staged_pool.tile([P, BANK], F32, name="staged")
                 turn = 2 if scalar_is_free else SCALAR_TURN
                 if (n * GROUPS_A_PIECE + i) % turn == turn - 1:
-                    nc.scalar.activation(staged[:], product[:], COPY)
+                    nc.scalar.activation(staged[:, i * BANK : (i + 1) * BANK], product[:], COPY)
                 else:
-                    nc.vector.tensor_copy(staged[:], product[:])
-                nc.sync.dma_start(out[b * P : (b + 1) * P, g * BANK : (g + 1) * BANK], staged[:])
+                    nc.vector.tensor_copy(staged[:, i * BANK : (i + 1) * BANK], product[:])
+            width = GROUPS_A_PIECE * BANK
+            nc.sync.dma_start(out[b * P : (b + 1) * P, k * width : (k + 1) * width], staged[:])
 
         for g in range(GROUPS):
             add_up(g)

@@ -14,14 +14,16 @@ ENTRIES, READ_IN = 1024, 256
 BANK = 512
 PIECE = 512
 BLOCKS = TOKENS // P
-PIECES_A_BLOCK = ENTRIES // PIECE
-GROUPS_A_PIECE = PIECE * READ_IN // (P * BANK)
-GROUPS = PIECES_A_BLOCK * GROUPS_A_PIECE
-TILES_A_GROUP = BANK // READ_IN
-LOOK_UPS = BLOCKS * PIECES_A_BLOCK
-FLIP_LAG = 2
-PRODUCT_LAG = 4
-SCALAR_TURN = 8
+PIECES = ENTRIES // PIECE
+LIST_TILES = ENTRIES // P
+TILES_A_PIECE = PIECE // P
+TILES_A_BANK = BANK // READ_IN
+BANKS_A_PIECE = TILES_A_PIECE // TILES_A_BANK
+LOOK_UPS = BLOCKS * PIECES
+TILES_A_ROUND = 2
+FLIP_LAG = 1
+PRODUCT_LAG = 3
+SHARED = 4
 
 FLOPS = 2 * TOKENS * ENTRIES * READ_IN
 
@@ -30,33 +32,25 @@ def tile_tiledsparseread_kernel(tc, x, v, offs, out):
     nc = tc.nc
     with (
         tc.tile_pool(name="held", bufs=1) as held,
-        tc.tile_pool(name="scratch", bufs=GROUPS) as scratch,
-        tc.tile_pool(name="picked", bufs=FLIP_LAG + 4) as picked_pool,
-        tc.tile_pool(name="flipped", bufs=PRODUCT_LAG - FLIP_LAG + 4) as flipped_pool,
+        tc.tile_pool(name="scratch", bufs=LIST_TILES) as scratch,
+        tc.tile_pool(name="picked", bufs=LOOK_UPS) as picked_pool,
+        tc.tile_pool(name="flipped", bufs=LOOK_UPS) as flipped_pool,
         tc.tile_pool(name="staged", bufs=8) as staged_pool,
-        tc.psum_pool(name="banks", bufs=8) as banks,
+        tc.psum_pool(name="sums", bufs=2) as sums_pool,
+        tc.psum_pool(name="turned", bufs=2) as turned_pool,
+        tc.psum_pool(name="product", bufs=4) as product_pool,
     ):
+        order = [(b, k) for k in range(PIECES) for b in range(BLOCKS)]
+
         offsets = held.tile([P, ENTRIES // 16], U16, name="offsets")
         nc.sync.dma_start(offsets[:], offs)
 
         tokens = [held.tile([P, FEATURES], F32, name=f"tokens{b}") for b in range(BLOCKS)]
-        raw = [held.tile([P, BANK], F32, name=f"raw{g}") for g in range(GROUPS)]
-
-        def load_tokens(b):
-            nc.sync.dma_start(tokens[b][:], x[b * P : (b + 1) * P, :])
-
-        def load_columns(k):
-            for g in range(k * GROUPS_A_PIECE, (k + 1) * GROUPS_A_PIECE):
-                rows = v[g * TILES_A_GROUP * P : (g + 1) * TILES_A_GROUP * P, :]
-                nc.sync.dma_start(
-                    raw[g][:].rearrange("t (h r) -> t h r", h=TILES_A_GROUP),
-                    rows.rearrange("(h t) r -> t h r", t=P),
-                )
-
+        raw = [held.tile([P, READ_IN], F32, name=f"raw{u}") for u in range(LIST_TILES)]
         for b in range(BLOCKS):
-            load_tokens(b)
-            if b < PIECES_A_BLOCK:
-                load_columns(b)
+            nc.sync.dma_start(tokens[b][:], x[b * P : (b + 1) * P, :])
+            for u in range(b * TILES_A_ROUND, min((b + 1) * TILES_A_ROUND, LIST_TILES)):
+                nc.sync.dma_start(raw[u][:], v[u * P : (u + 1) * P, :])
 
         identity = held.tile([P, P], BF16, name="identity")
         make_identity(nc, identity[:])
@@ -65,24 +59,21 @@ def tile_tiledsparseread_kernel(tc, x, v, offs, out):
         unused = held.tile([P, 1], F32, name="unused")
         nc.scalar.activation(unused[:], ones[:, 0:1], INVERSE_ROOT)
 
-        sums = {}
         unit = {}
 
-        def add_up(g):
-            squares = scratch.tile([P, BANK], F32, name="squares")
-            nc.vector.tensor_tensor(squares[:], raw[g][:], raw[g][:], MULT)
-            sums[g] = banks.tile([P, BANK], F32, name="sums", tag="bank")
-            nc.tensor.matmul(sums[g][:], ones[:], squares[:], start=True, stop=True)
-
-        def scale(k):
-            for g in range(k * GROUPS_A_PIECE, (k + 1) * GROUPS_A_PIECE):
-                inverse = scratch.tile([P, BANK], F32, name="inverse")
-                nc.scalar.activation(inverse[:], sums[g][:], INVERSE_ROOT)
-                unit[g] = held.tile([P, BANK], BF16, name=f"unit{g}")
-                nc.gpsimd.tensor_tensor(unit[g][:], raw[g][:], inverse[:], MULT)
+        def normalise(u):
+            engine = nc.vector if u < TILES_A_PIECE else nc.gpsimd
+            squares = scratch.tile([P, READ_IN], F32, name="squares")
+            engine.tensor_tensor(squares[:], raw[u][:], raw[u][:], MULT)
+            sums = sums_pool.tile([P, READ_IN], F32, name="sums")
+            nc.tensor.matmul(sums[:], ones[:], squares[:], start=True, stop=True)
+            inverse = scratch.tile([P, READ_IN], F32, name="inverse")
+            nc.scalar.activation(inverse[:], sums[:], INVERSE_ROOT)
+            unit[u] = held.tile([P, READ_IN], BF16, name=f"unit{u}")
+            engine.tensor_tensor(unit[u][:], raw[u][:], inverse[:], MULT)
 
         def look_up(n):
-            b, k = n // PIECES_A_BLOCK, n % PIECES_A_BLOCK
+            b, k = order[n]
             picked = picked_pool.tile([P, PIECE], F32, name="picked")
             entries = offsets[:, k * PIECE // 16 : (k + 1) * PIECE // 16]
             nc.scalar.activation(picked[:], tokens[b][:].indirect(entries), COPY)
@@ -90,8 +81,8 @@ def tile_tiledsparseread_kernel(tc, x, v, offs, out):
 
         def flip(picked):
             halves = picked[:].bitcast(BF16).rearrange("c (j half) -> c j half", half=2)
-            turned = banks.tile([P, PIECE], BF16, name="turned", tag="bank")
-            for j in range(PIECE // P):
+            turned = turned_pool.tile([P, PIECE], BF16, name="turned")
+            for j in range(TILES_A_PIECE):
                 nc.tensor.transpose(
                     turned[:, j * P : (j + 1) * P], halves[:, j * P : (j + 1) * P, 1], identity[:]
                 )
@@ -99,40 +90,35 @@ def tile_tiledsparseread_kernel(tc, x, v, offs, out):
             nc.vector.tensor_copy(flipped[:], turned[:])
             return flipped
 
-        def project(n, flipped, scalar_is_free):
-            b, k = n // PIECES_A_BLOCK, n % PIECES_A_BLOCK
-            staged = staged_pool.tile([P, GROUPS_A_PIECE * BANK], F32, name="staged")
-            for i in range(GROUPS_A_PIECE):
-                g = k * GROUPS_A_PIECE + i
-                product = banks.tile([P, BANK], F32, name="product", tag="bank")
-                for h in range(TILES_A_GROUP):
-                    j = i * TILES_A_GROUP + h
+        def project(n, flipped):
+            b, k = order[n]
+            staged = staged_pool.tile([P, BANKS_A_PIECE * BANK], F32, name="staged")
+            for i in range(BANKS_A_PIECE):
+                product = product_pool.tile([P, BANK], F32, name="product")
+                for h in range(TILES_A_BANK):
+                    j = i * TILES_A_BANK + h
                     nc.tensor.matmul(
                         product[:, h * READ_IN : (h + 1) * READ_IN],
                         flipped[:, j * P : (j + 1) * P],
-                        unit[g][:, h * READ_IN : (h + 1) * READ_IN],
+                        unit[k * TILES_A_PIECE + j][:],
                         start=True,
                         stop=True,
                     )
-                turn = 2 if scalar_is_free else SCALAR_TURN
-                if (n * GROUPS_A_PIECE + i) % turn == turn - 1:
+                if n >= LOOK_UPS - SHARED and i % 2 == 1:
                     nc.scalar.activation(staged[:, i * BANK : (i + 1) * BANK], product[:], COPY)
                 else:
                     nc.vector.tensor_copy(staged[:, i * BANK : (i + 1) * BANK], product[:])
-            width = GROUPS_A_PIECE * BANK
+            width = BANKS_A_PIECE * BANK
             nc.sync.dma_start(out[b * P : (b + 1) * P, k * width : (k + 1) * width], staged[:])
-
-        for g in range(GROUPS):
-            add_up(g)
 
         picked_tiles = {}
         flipped_tiles = {}
         for r in range(LOOK_UPS + PRODUCT_LAG):
             if r >= PRODUCT_LAG:
-                project(r - PRODUCT_LAG, flipped_tiles[r - PRODUCT_LAG], r >= LOOK_UPS)
+                project(r - PRODUCT_LAG, flipped_tiles[r - PRODUCT_LAG])
             if FLIP_LAG <= r < LOOK_UPS + FLIP_LAG:
                 flipped_tiles[r - FLIP_LAG] = flip(picked_tiles[r - FLIP_LAG])
+            for u in range(r * TILES_A_ROUND, min((r + 1) * TILES_A_ROUND, LIST_TILES)):
+                normalise(u)
             if r < LOOK_UPS:
                 picked_tiles[r] = look_up(r)
-            if 1 <= r <= PIECES_A_BLOCK:
-                scale(r - 1)

@@ -23,7 +23,7 @@ LOOK_UPS = BLOCKS * PIECES
 TILES_A_ROUND = 2
 FLIP_LAG = 1
 PRODUCT_LAG = 3
-SHARED = 4
+SHARED = 6
 
 FLOPS = 2 * TOKENS * ENTRIES * READ_IN
 
@@ -33,8 +33,8 @@ def tile_tiledsparseread_kernel(tc, x, v, offs, out):
     with (
         tc.tile_pool(name="held", bufs=1) as held,
         tc.tile_pool(name="scratch", bufs=LIST_TILES) as scratch,
-        tc.tile_pool(name="picked", bufs=LOOK_UPS) as picked_pool,
-        tc.tile_pool(name="flipped", bufs=LOOK_UPS) as flipped_pool,
+        tc.tile_pool(name="picked", bufs=4) as picked_pool,
+        tc.tile_pool(name="flipped", bufs=3) as flipped_pool,
         tc.tile_pool(name="staged", bufs=8) as staged_pool,
         tc.psum_pool(name="sums", bufs=2) as sums_pool,
         tc.psum_pool(name="turned", bufs=2) as turned_pool,

@@ -47,10 +47,15 @@ def tile_tiledsparseread_kernel(tc, x, v, offs, out):
 
         tokens = [held.tile([P, FEATURES], F32, name=f"tokens{b}") for b in range(BLOCKS)]
         raw = [held.tile([P, READ_IN], F32, name=f"raw{u}") for u in range(LIST_TILES)]
+
+        def load_columns(u):
+            nc.sync.dma_start(raw[u][:], v[u * P : (u + 1) * P, :])
+
+        load_columns(0)
         for b in range(BLOCKS):
             nc.sync.dma_start(tokens[b][:], x[b * P : (b + 1) * P, :])
-            for u in range(b * TILES_A_ROUND, min((b + 1) * TILES_A_ROUND, LIST_TILES)):
-                nc.sync.dma_start(raw[u][:], v[u * P : (u + 1) * P, :])
+            for u in range(max(b * TILES_A_ROUND, 1), min((b + 1) * TILES_A_ROUND, LIST_TILES)):
+                load_columns(u)
 
         identity = held.tile([P, P], BF16, name="identity")
         make_identity(nc, identity[:])

@@ -66,16 +66,24 @@ def tile_tiledsparseread_kernel(tc, x, v, offs, out):
 
         unit = {}
 
-        def normalise(u):
-            engine = nc.vector if u < TILES_A_PIECE else nc.gpsimd
-            squares = scratch.tile([P, READ_IN], F32, name="squares")
-            engine.tensor_tensor(squares[:], raw[u][:], raw[u][:], MULT)
-            sums = sums_pool.tile([P, READ_IN], F32, name="sums")
-            nc.tensor.matmul(sums[:], ones[:], squares[:], start=True, stop=True)
-            inverse = scratch.tile([P, READ_IN], F32, name="inverse")
+        def normalise(g):
+            engine = nc.vector if g < BANKS_A_PIECE else nc.gpsimd
+            sums = sums_pool.tile([P, BANK], F32, name="sums")
+            for h in range(TILES_A_BANK):
+                u = g * TILES_A_BANK + h
+                squares = scratch.tile([P, READ_IN], F32, name="squares")
+                engine.tensor_tensor(squares[:], raw[u][:], raw[u][:], MULT)
+                nc.tensor.matmul(
+                    sums[:, h * READ_IN : (h + 1) * READ_IN], ones[:], squares[:], start=True, stop=True
+                )
+            inverse = scratch.tile([P, BANK], F32, name="inverse")
             nc.scalar.activation(inverse[:], sums[:], INVERSE_ROOT)
-            unit[u] = held.tile([P, READ_IN], BF16, name=f"unit{u}")
-            engine.tensor_tensor(unit[u][:], raw[u][:], inverse[:], MULT)
+            for h in range(TILES_A_BANK):
+                u = g * TILES_A_BANK + h
+                unit[u] = held.tile([P, READ_IN], BF16, name=f"unit{u}")
+                engine.tensor_tensor(
+                    unit[u][:], raw[u][:], inverse[:, h * READ_IN : (h + 1) * READ_IN], MULT
+                )
 
         def look_up(n):
             b, k = order[n]
@@ -123,7 +131,7 @@ def tile_tiledsparseread_kernel(tc, x, v, offs, out):
                 project(r - PRODUCT_LAG, flipped_tiles[r - PRODUCT_LAG])
             if FLIP_LAG <= r < LOOK_UPS + FLIP_LAG:
                 flipped_tiles[r - FLIP_LAG] = flip(picked_tiles[r - FLIP_LAG])
-            for u in range(r * TILES_A_ROUND, min((r + 1) * TILES_A_ROUND, LIST_TILES)):
-                normalise(u)
+            if r < LIST_TILES // TILES_A_BANK:
+                normalise(r)
             if r < LOOK_UPS:
                 picked_tiles[r] = look_up(r)

@@ -23,7 +23,8 @@ LOOK_UPS = BLOCKS * PIECES
 TILES_A_ROUND = 2
 FLIP_LAG = 1
 PRODUCT_LAG = 3
-SHARED = 6
+SHARED = 2
+FIRST_SCALAR_FLIP = 3
 
 FLOPS = 2 * TOKENS * ENTRIES * READ_IN
 
@@ -92,7 +93,7 @@ def tile_tiledsparseread_kernel(tc, x, v, offs, out):
             nc.scalar.activation(picked[:], tokens[b][:].indirect(entries), COPY)
             return picked
 
-        def flip(picked):
+        def flip(n, picked):
             halves = picked[:].bitcast(BF16).rearrange("c (j half) -> c j half", half=2)
             turned = turned_pool.tile([P, PIECE], BF16, name="turned")
             for j in range(TILES_A_PIECE):
@@ -100,7 +101,10 @@ def tile_tiledsparseread_kernel(tc, x, v, offs, out):
                     turned[:, j * P : (j + 1) * P], halves[:, j * P : (j + 1) * P, 1], identity[:]
                 )
             flipped = flipped_pool.tile([P, PIECE], BF16, name="flipped")
-            nc.vector.tensor_copy(flipped[:], turned[:])
+            if n >= FIRST_SCALAR_FLIP and n % 2 == 1:
+                nc.scalar.copy(flipped[:], turned[:])
+            else:
+                nc.vector.tensor_copy(flipped[:], turned[:])
             return flipped
 
         def project(n, flipped):
@@ -130,7 +134,7 @@ def tile_tiledsparseread_kernel(tc, x, v, offs, out):
             if r >= PRODUCT_LAG:
                 project(r - PRODUCT_LAG, flipped_tiles[r - PRODUCT_LAG])
             if FLIP_LAG <= r < LOOK_UPS + FLIP_LAG:
-                flipped_tiles[r - FLIP_LAG] = flip(picked_tiles[r - FLIP_LAG])
+                flipped_tiles[r - FLIP_LAG] = flip(r - FLIP_LAG, picked_tiles[r - FLIP_LAG])
             if r < LIST_TILES // TILES_A_BANK:
                 normalise(r)
             if r < LOOK_UPS:

import concourse.mybir as mybir
from concourse.masks import make_identity

F32 = mybir.dt.float32
BF16 = mybir.dt.bfloat16
U16 = mybir.dt.uint16
COPY = mybir.ActivationFunctionType.Copy
INVERSE_ROOT = mybir.ActivationFunctionType.Abs_reciprocal_sqrt
MULT = mybir.AluOpType.mult

P = 128
TOKENS, FEATURES = 1024, 512
ENTRIES, READ_IN = 1024, 256
BANK = 512
PIECE = 512
BLOCKS = TOKENS // P
PIECES = ENTRIES // PIECE
LIST_TILES = ENTRIES // P
TILES_A_PIECE = PIECE // P
TILES_A_BANK = BANK // READ_IN
BANKS_A_PIECE = TILES_A_PIECE // TILES_A_BANK
LOOK_UPS = BLOCKS * PIECES
TILES_A_ROUND = 2
FLIP_LAG = 1
PRODUCT_LAG = 3
SHARED = 2
FIRST_SCALAR_FLIP = 3

FLOPS = 2 * TOKENS * ENTRIES * READ_IN


def tile_tiledsparseread_kernel(tc, x, v, offs, out):
    nc = tc.nc
    with (
        tc.tile_pool(name="held", bufs=1) as held,
        tc.tile_pool(name="scratch", bufs=LIST_TILES) as scratch,
        tc.tile_pool(name="picked", bufs=4) as picked_pool,
        tc.tile_pool(name="flipped", bufs=3) as flipped_pool,
        tc.tile_pool(name="staged", bufs=8) as staged_pool,
        tc.psum_pool(name="sums", bufs=2) as sums_pool,
        tc.psum_pool(name="turned", bufs=2) as turned_pool,
        tc.psum_pool(name="product", bufs=4) as product_pool,
    ):
        order = [(b, k) for k in range(PIECES) for b in range(BLOCKS)]

        offsets = held.tile([P, ENTRIES // 16], U16, name="offsets")
        nc.sync.dma_start(offsets[:], offs)

        tokens = [held.tile([P, FEATURES], F32, name=f"tokens{b}") for b in range(BLOCKS)]
        raw = [held.tile([P, READ_IN], F32, name=f"raw{u}") for u in range(LIST_TILES)]

        def load_columns(u):
            nc.sync.dma_start(raw[u][:], v[u * P : (u + 1) * P, :])

        load_columns(0)
        for b in range(BLOCKS):
            nc.sync.dma_start(tokens[b][:], x[b * P : (b + 1) * P, :])
            for u in range(max(b * TILES_A_ROUND, 1), min((b + 1) * TILES_A_ROUND, LIST_TILES)):
                load_columns(u)

        identity = held.tile([P, P], BF16, name="identity")
        make_identity(nc, identity[:])
        ones = held.tile([P, P], F32, name="ones")
        nc.vector.memset(ones[:], 1.0)
        unused = held.tile([P, 1], F32, name="unused")
        nc.scalar.activation(unused[:], ones[:, 0:1], INVERSE_ROOT)

        unit = {}

        def normalise(g):
            engine = nc.vector if g < BANKS_A_PIECE else nc.gpsimd
            sums = sums_pool.tile([P, BANK], F32, name="sums")
            for h in range(TILES_A_BANK):
                u = g * TILES_A_BANK + h
                squares = scratch.tile([P, READ_IN], F32, name="squares")
                engine.tensor_tensor(squares[:], raw[u][:], raw[u][:], MULT)
                nc.tensor.matmul(
                    sums[:, h * READ_IN : (h + 1) * READ_IN], ones[:], squares[:], start=True, stop=True
                )
            inverse = scratch.tile([P, BANK], F32, name="inverse")
            nc.scalar.activation(inverse[:], sums[:], INVERSE_ROOT)
            for h in range(TILES_A_BANK):
                u = g * TILES_A_BANK + h
                unit[u] = held.tile([P, READ_IN], BF16, name=f"unit{u}")
                engine.tensor_tensor(
                    unit[u][:], raw[u][:], inverse[:, h * READ_IN : (h + 1) * READ_IN], MULT
                )

        def look_up(n):
            b, k = order[n]
            picked = picked_pool.tile([P, PIECE], F32, name="picked")
            entries = offsets[:, k * PIECE // 16 : (k + 1) * PIECE // 16]
            nc.scalar.activation(picked[:], tokens[b][:].indirect(entries), COPY)
            return picked

        def flip(n, picked):
            halves = picked[:].bitcast(BF16).rearrange("c (j half) -> c j half", half=2)
            turned = turned_pool.tile([P, PIECE], BF16, name="turned")
            for j in range(TILES_A_PIECE):
                nc.tensor.transpose(
                    turned[:, j * P : (j + 1) * P], halves[:, j * P : (j + 1) * P, 1], identity[:]
                )
            flipped = flipped_pool.tile([P, PIECE], BF16, name="flipped")
            if n >= FIRST_SCALAR_FLIP and n % 2 == 1:
                nc.scalar.copy(flipped[:], turned[:])
            else:
                nc.vector.tensor_copy(flipped[:], turned[:])
            return flipped

        def project(n, flipped):
            b, k = order[n]
            staged = staged_pool.tile([P, BANKS_A_PIECE * BANK], F32, name="staged")
            for i in range(BANKS_A_PIECE):
                product = product_pool.tile([P, BANK], F32, name="product")
                for h in range(TILES_A_BANK):
                    j = i * TILES_A_BANK + h
                    nc.tensor.matmul(
                        product[:, h * READ_IN : (h + 1) * READ_IN],
                        flipped[:, j * P : (j + 1) * P],
                        unit[k * TILES_A_PIECE + j][:],
                        start=True,
                        stop=True,
                    )
                if n >= LOOK_UPS - SHARED and i % 2 == 1:
                    nc.scalar.activation(staged[:, i * BANK : (i + 1) * BANK], product[:], COPY)
                else:
                    nc.vector.tensor_copy(staged[:, i * BANK : (i + 1) * BANK], product[:])
            width = BANKS_A_PIECE * BANK
            nc.sync.dma_start(out[b * P : (b + 1) * P, k * width : (k + 1) * width], staged[:])

        picked_tiles = {}
        flipped_tiles = {}
        for r in range(LOOK_UPS + PRODUCT_LAG):
            if r >= PRODUCT_LAG:
                project(r - PRODUCT_LAG, flipped_tiles[r - PRODUCT_LAG])
            if FLIP_LAG <= r < LOOK_UPS + FLIP_LAG:
                flipped_tiles[r - FLIP_LAG] = flip(r - FLIP_LAG, picked_tiles[r - FLIP_LAG])
            if r < LIST_TILES // TILES_A_BANK:
                normalise(r)
            if r < LOOK_UPS:
                picked_tiles[r] = look_up(r)
